import numpy as np
import ml_dtypes


def mxq(x, axis, fmt="e4m3"):
    dtype, down = {"e4m3": (ml_dtypes.float8_e4m3fn, 7), "e5m2": (ml_dtypes.float8_e5m2, 14)}[fmt]
    v = np.moveaxis(np.asarray(x, np.float32).astype(ml_dtypes.bfloat16).astype(np.float64), axis, -1)
    blocks = v.reshape(v.shape[:-1] + (-1, 32))
    amax = np.abs(blocks).max(-1, keepdims=True)
    byte = np.maximum(np.where(amax > 0, np.frexp(amax)[1] - 1 + 127, 0) - down, 1)
    scale = np.exp2(byte - 127.0)
    codes = (blocks / scale).astype(np.float32).astype(dtype).astype(np.float64)
    return np.moveaxis((codes * scale).reshape(v.shape), -1, axis)


WIDE = False


def mx_kscale(k):
    if not WIDE:
        return np.ones(k)
    levels = np.array([10, -10, 5, -5, 0])
    a = np.random.permutation(np.resize(levels, k // 512 * 4)).reshape(k // 512, 4)
    idx = np.arange(k)
    return np.exp2(a[idx // 512, idx % 128 // 32])


BF16 = ml_dtypes.bfloat16


def bf(x):
    return np.asarray(x, np.float32).astype(BF16)


def f64(x):
    return np.asarray(x).astype(np.float64)


E2M1 = np.array([0.0, 0.5, 1.0, 1.5, 2.0, 3.0, 4.0, 6.0, -0.0, -0.5, -1.0, -1.5, -2.0, -3.0, -4.0, -6.0])


def pack_weight(w, fmt):
    k, n = w.shape
    w = f64(bf(w)).reshape(k // 32, 32, n)
    amax = np.abs(w).max(1)
    if fmt == "e4m3":
        byte = np.frexp(amax)[1] - 1 + 127 - 7
    else:
        mant, ex = np.frexp(amax / 6.0)
        byte = np.where(mant > 0.5, ex, ex - 1) + 127
    byte = np.clip(np.where(amax > 0, byte, 1), 1, 254)
    scaled = (w * np.exp2(127.0 - byte)[:, None, :]).reshape(k, n).astype(np.float32)
    by_word = np.ascontiguousarray(scaled.reshape(k // 512, 128, 4, n).transpose(0, 1, 3, 2))
    if fmt == "e4m3":
        words = by_word.astype(ml_dtypes.float8_e4m3fn).view(np.uint8)
    else:
        c = by_word.astype(ml_dtypes.float4_e2m1fn).view(np.uint8) & 0xF
        words = c[..., 0::2] | (c[..., 1::2] << 4)
    return np.ascontiguousarray(words), np.ascontiguousarray(byte.astype(np.uint8).reshape(k // 512, 16, n))


def unpack_weight(words, scales, fmt):
    g, p, n, _ = words.shape
    if fmt == "e4m3":
        vals = np.ascontiguousarray(words).view(ml_dtypes.float8_e4m3fn).astype(np.float64)
    else:
        nib = np.empty((g, p, n, 4), np.uint8)
        nib[..., 0::2] = words & 0xF
        nib[..., 1::2] = words >> 4
        vals = E2M1[nib]
    vals = vals * np.repeat(np.exp2(scales.astype(np.float64) - 127.0), 8, axis=1)[..., None]
    return vals.transpose(0, 1, 3, 2).reshape(g * 512, n)


T, D, E = 128, 6144, 3072


def setup_inputs():
    s = mx_kscale(D)
    hidden_states = bf(np.random.standard_normal((T, D)) * s)
    weight = np.random.standard_normal((E, D)) * 1.0 / np.sqrt(D) / s[None, :]
    words, scales = pack_weight(np.ascontiguousarray(weight.T), "e4m3")
    return {"hidden_states": hidden_states,
            "weight_words": words,
            "weight_scales": scales}


def reference(hidden_states, weight_words, weight_scales):
    logits = mxq(f64(hidden_states), 1, "e4m3") @ unpack_weight(weight_words, weight_scales, "e4m3")
    return logits

@@ -1,0 +1,123 @@
+from contextlib import ExitStack
+
+import concourse.mybir as mybir
+from concourse.masks import make_identity
+
+F32 = mybir.dt.float32
+BF16 = mybir.dt.bfloat16
+I32 = mybir.dt.int32
+U32 = mybir.dt.uint32
+U8 = mybir.dt.uint8
+FP8X4 = mybir.dt.float8_e4m3fn_x4
+
+P = 128
+T, D, E = 128, 6144, 3072
+K_PASS = 512
+G = D // K_PASS
+N_TILE = 512
+NCH = E // N_TILE
+
+FLOPS = 2 * T * D * E
+
+
+def tile_longcatrouter_w_kernel(tc, hidden_states, weight_words, weight_scales, out):
+    nc = tc.nc
+    with ExitStack() as ctx:
+        keep = ctx.enter_context(tc.tile_pool(name="keep", bufs=1))
+        psum = ctx.enter_context(tc.psum_pool(name="psum", bufs=1))
+        ctx.enter_context(tc.manual_schedule())
+
+        planes = keep.tile([P, 3 * E], U8, align_bytes=64)
+        nc.vector.memset(planes[:].bitcast(I32), 0)
+        ident = keep.tile([P, P], F32)
+        make_identity(nc, ident[:])
+
+        x_sb = keep.tile([P, D], BF16, align_bytes=64)
+        nc.sync.dma_start(out=x_sb[:], in_=hidden_states)
+
+        for quads in ((2, 3), (0, 1)):
+            for j in range(3):
+                for q in quads:
+                    nc.sync.dma_start(
+                        out=planes[32 * q : 32 * q + 16, j * E : (j + 1) * E].bitcast(I32),
+                        in_=weight_scales[4 * j : 4 * j + 4, 4 * q : 4 * q + 4, :].bitcast(I32),
+                    )
+
+        w = []
+        for g in range(G - 1):
+            wt = keep.tile([P, E], U32, name="w%d" % g, align_bytes=64)
+            nc.sync.dma_start(
+                out=wt[:].bitcast(I32),
+                in_=weight_words[g].rearrange("p n t -> p (n t)").bitcast(I32),
+            )
+            w.append(wt)
+        w_last = []
+        for c in range(NCH):
+            wt = keep.tile([P, N_TILE], U32, name="wl%d" % c, align_bytes=64)
+            nc.sync.dma_start(
+                out=wt[:].bitcast(I32),
+                in_=weight_words[G - 1, :, c * N_TILE : (c + 1) * N_TILE, :]
+                .rearrange("p n t -> p (n t)")
+                .bitcast(I32),
+            )
+            w_last.append(wt)
+
+        xw = x_sb[:].bitcast(F32)
+        grouped = keep.tile([P, D], BF16, align_bytes=64)
+        gw = grouped[:].bitcast(F32)
+        x_codes = keep.tile([P, G * P], U32, align_bytes=64)
+        x_scales = keep.tile([P, G * P], U8, align_bytes=64)
+
+        def quantise(h):
+            nc.vector.quantize_mx(
+                out=x_codes[:, 512 * h : 512 * (h + 1)].bitcast(FP8X4),
+                scales=x_scales[:, 512 * h : 512 * (h + 1)],
+                in_=grouped[:, 2048 * h : 2048 * (h + 1)],
+            )
+
+        for b in range(6):
+            tr = psum.tile([P, 512], F32, name="tr%d" % b, tag="tr%d" % (b % 2))
+            for i in range(4):
+                g = 2 * b + i // 2
+                u = i % 2
+                nc.tensor.transpose(
+                    tr[:, 128 * i : 128 * (i + 1)],
+                    xw[:, 256 * g + u : 256 * (g + 1) : 2],
+                    ident[:],
+                )
+            src = tr[:].rearrange("p (g u t) -> p g t u", g=2, u=2)
+            dst = gw[:, 512 * b : 512 * (b + 1)].rearrange("p (g t u) -> p g t u", g=2, u=2)
+            if b % 2 == 0:
+                nc.vector.tensor_copy(out=dst, in_=src)
+            else:
+                nc.scalar.copy(out=dst, in_=src)
+            if b == 3 or b == 5:
+                quantise((b - 3) // 2)
+        quantise(2)
+
+        acc = [psum.tile([P, N_TILE], F32, name="acc%d" % c) for c in range(NCH)]
+        for g in range(G):
+            i = g % 4
+            j = g // 4
+            for c in range(NCH):
+                if g < G - 1:
+                    rhs = w[g][:, c * N_TILE : (c + 1) * N_TILE]
+                else:
+                    rhs = w_last[c][:]
+                nc.tensor.matmul_mx(
+                    out=acc[c][:],
+                    lhsT=x_codes[:, P * g : P * (g + 1)].bitcast(FP8X4),
+                    lhsT_scale=x_scales[:, P * g : P * (g + 1)],
+                    rhs=rhs.bitcast(FP8X4),
+                    rhs_scale=planes[4 * i : P, j * E + c * N_TILE : j * E + (c + 1) * N_TILE],
+                    start=(g == 0),
+                    stop=(g == G - 1),
+                )
+
+        for c in range(NCH):
+            o = keep.tile([P, N_TILE], F32, name="o%d" % c)
+            if c % 2 == 0:
+                nc.vector.tensor_copy(out=o[:], in_=acc[c][:])
+            else:
+                nc.scalar.copy(out=o[:], in_=acc[c][:])
+            nc.sync.dma_start(out=out[:, c * N_TILE : (c + 1) * N_TILE], in_=o[:])

@@ -35,13 +35,12 @@ def tile_longcatrouter_w_kernel(tc, hidden_states, weight_words, weight_scales, 
         x_sb = keep.tile([P, D], BF16, align_bytes=64)
         nc.sync.dma_start(out=x_sb[:], in_=hidden_states)
 
-        for quads in ((2, 3), (0, 1)):
-            for j in range(3):
-                for q in quads:
-                    nc.sync.dma_start(
-                        out=planes[32 * q : 32 * q + 16, j * E : (j + 1) * E].bitcast(I32),
-                        in_=weight_scales[4 * j : 4 * j + 4, 4 * q : 4 * q + 4, :].bitcast(I32),
-                    )
+        for j in range(3):
+            for q in (0, 2, 1, 3):
+                nc.gpsimd.dma_start(
+                    out=planes[32 * q : 32 * q + 16, j * E : (j + 1) * E].bitcast(F32),
+                    in_=weight_scales[4 * j : 4 * j + 4, 4 * q : 4 * q + 4, :].bitcast(F32),
+                )
 
         w = []
         for g in range(G - 1):

@@ -14,8 +14,11 @@ P = 128
 T, D, E = 128, 6144, 3072
 K_PASS = 512
 G = D // K_PASS
-N_TILE = 512
-NCH = E // N_TILE
+
+BANKS = ((0, 512), (512, 512), (1024, 512), (1536, 512), (2048, 512), (2560, 256), (2816, 128), (2944, 128))
+N_WIDE = 5
+SPLIT = 2560
+G_WHOLE = 8
 
 FLOPS = 2 * T * D * E
 
@@ -35,31 +38,36 @@ def tile_longcatrouter_w_kernel(tc, hidden_states, weight_words, weight_scales, 
         x_sb = keep.tile([P, D], BF16, align_bytes=64)
         nc.sync.dma_start(out=x_sb[:], in_=hidden_states)
 
-        for j in range(3):
-            for q in (0, 2, 1, 3):
-                nc.gpsimd.dma_start(
-                    out=planes[32 * q : 32 * q + 16, j * E : (j + 1) * E].bitcast(F32),
-                    in_=weight_scales[4 * j : 4 * j + 4, 4 * q : 4 * q + 4, :].bitcast(F32),
-                )
+        for quads in ((2, 3), (0, 1)):
+            for j in range(3):
+                for q in quads:
+                    nc.sync.dma_start(
+                        out=planes[32 * q : 32 * q + 16, j * E : (j + 1) * E].bitcast(I32),
+                        in_=weight_scales[4 * j : 4 * j + 4, 4 * q : 4 * q + 4, :].bitcast(I32),
+                    )
 
-        w = []
-        for g in range(G - 1):
-            wt = keep.tile([P, E], U32, name="w%d" % g, align_bytes=64)
+        def load_words(name, g, c0, width):
+            wt = keep.tile([P, width], U32, name=name, align_bytes=64)
             nc.sync.dma_start(
                 out=wt[:].bitcast(I32),
-                in_=weight_words[g].rearrange("p n t -> p (n t)").bitcast(I32),
+                in_=weight_words[g, :, c0 : c0 + width, :].rearrange("p n t -> p (n t)").bitcast(I32),
             )
-            w.append(wt)
-        w_last = []
-        for c in range(NCH):
-            wt = keep.tile([P, N_TILE], U32, name="wl%d" % c, align_bytes=64)
-            nc.sync.dma_start(
-                out=wt[:].bitcast(I32),
-                in_=weight_words[G - 1, :, c * N_TILE : (c + 1) * N_TILE, :]
-                .rearrange("p n t -> p (n t)")
-                .bitcast(I32),
-            )
-            w_last.append(wt)
+            return wt
+
+        whole = {}
+        wide = {}
+        narrow = {}
+        last = {}
+        for g in range(G_WHOLE):
+            whole[g] = load_words("w%d" % g, g, 0, E)
+        for g in range(G_WHOLE, G - 1):
+            wide[g] = load_words("wa%d" % g, g, 0, SPLIT)
+        for b in range(N_WIDE):
+            last[b] = load_words("wl%d" % b, G - 1, BANKS[b][0], BANKS[b][1])
+        for g in range(G_WHOLE, G - 1):
+            narrow[g] = load_words("wb%d" % g, g, SPLIT, E - SPLIT)
+        for b in range(N_WIDE, len(BANKS)):
+            last[b] = load_words("wl%d" % b, G - 1, BANKS[b][0], BANKS[b][1])
 
         xw = x_sb[:].bitcast(F32)
         grouped = keep.tile([P, D], BF16, align_bytes=64)
@@ -75,7 +83,7 @@ def tile_longcatrouter_w_kernel(tc, hidden_states, weight_words, weight_scales, 
             )
 
         for b in range(6):
-            tr = psum.tile([P, 512], F32, name="tr%d" % b, tag="tr%d" % (b % 2))
+            tr = psum.tile([P, 512], F32, name="tr%d" % b, tag="b%d" % (6 + b % 2))
             for i in range(4):
                 g = 2 * b + i // 2
                 u = i % 2
@@ -94,29 +102,47 @@ def tile_longcatrouter_w_kernel(tc, hidden_states, weight_words, weight_scales, 
                 quantise((b - 3) // 2)
         quantise(2)
 
-        acc = [psum.tile([P, N_TILE], F32, name="acc%d" % c) for c in range(NCH)]
-        for g in range(G):
+        acc = [
+            psum.tile([P, BANKS[b][1]], F32, name="acc%d" % b, tag="b%d" % b) for b in range(len(BANKS))
+        ]
+
+        def mx_pass(g, b):
+            c0, width = BANKS[b]
+            if g < G_WHOLE:
+                rhs = whole[g][:, c0 : c0 + width]
+            elif g == G - 1:
+                rhs = last[b][:]
+            elif b < N_WIDE:
+                rhs = wide[g][:, c0 : c0 + width]
+            else:
+                rhs = narrow[g][:, c0 - SPLIT : c0 - SPLIT + width]
             i = g % 4
             j = g // 4
-            for c in range(NCH):
-                if g < G - 1:
-                    rhs = w[g][:, c * N_TILE : (c + 1) * N_TILE]
-                else:
-                    rhs = w_last[c][:]
-                nc.tensor.matmul_mx(
-                    out=acc[c][:],
-                    lhsT=x_codes[:, P * g : P * (g + 1)].bitcast(FP8X4),
-                    lhsT_scale=x_scales[:, P * g : P * (g + 1)],
-                    rhs=rhs.bitcast(FP8X4),
-                    rhs_scale=planes[4 * i : P, j * E + c * N_TILE : j * E + (c + 1) * N_TILE],
-                    start=(g == 0),
-                    stop=(g == G - 1),
-                )
+            nc.tensor.matmul_mx(
+                out=acc[b][:],
+                lhsT=x_codes[:, P * g : P * (g + 1)].bitcast(FP8X4),
+                lhsT_scale=x_scales[:, P * g : P * (g + 1)],
+                rhs=rhs.bitcast(FP8X4),
+                rhs_scale=planes[4 * i : P, j * E + c0 : j * E + c0 + width],
+                start=(g == 0),
+                stop=(g == G - 1),
+            )
 
-        for c in range(NCH):
-            o = keep.tile([P, N_TILE], F32, name="o%d" % c)
-            if c % 2 == 0:
-                nc.vector.tensor_copy(out=o[:], in_=acc[c][:])
+        for g in range(G_WHOLE):
+            for b in range(len(BANKS)):
+                mx_pass(g, b)
+        for g in range(G_WHOLE, G):
+            for b in range(N_WIDE):
+                mx_pass(g, b)
+        for g in range(G_WHOLE, G):
+            for b in range(N_WIDE, len(BANKS)):
+                mx_pass(g, b)
+
+        for b in range(len(BANKS)):
+            c0, width = BANKS[b]
+            o = keep.tile([P, width], F32, name="o%d" % b)
+            if b % 2 == 0:
+                nc.vector.tensor_copy(out=o[:], in_=acc[b][:])
             else:
-                nc.scalar.copy(out=o[:], in_=acc[c][:])
-            nc.sync.dma_start(out=out[:, c * N_TILE : (c + 1) * N_TILE], in_=o[:])
+                nc.scalar.copy(out=o[:], in_=acc[b][:])
+            nc.sync.dma_start(out=out[:, c0 : c0 + width], in_=o[:])

from contextlib import ExitStack

import concourse.mybir as mybir
from concourse.masks import make_identity

F32 = mybir.dt.float32
BF16 = mybir.dt.bfloat16
I32 = mybir.dt.int32
U32 = mybir.dt.uint32
U8 = mybir.dt.uint8
FP8X4 = mybir.dt.float8_e4m3fn_x4

P = 128
T, D, E = 128, 6144, 3072
K_PASS = 512
G = D // K_PASS

BANKS = ((0, 512), (512, 512), (1024, 512), (1536, 512), (2048, 512), (2560, 256), (2816, 128), (2944, 128))
N_WIDE = 5
SPLIT = 2560
G_WHOLE = 8

FLOPS = 2 * T * D * E


def tile_longcatrouter_w_kernel(tc, hidden_states, weight_words, weight_scales, out):
    nc = tc.nc
    with ExitStack() as ctx:
        keep = ctx.enter_context(tc.tile_pool(name="keep", bufs=1))
        psum = ctx.enter_context(tc.psum_pool(name="psum", bufs=1))
        ctx.enter_context(tc.manual_schedule())

        planes = keep.tile([P, 3 * E], U8, align_bytes=64)
        nc.vector.memset(planes[:].bitcast(I32), 0)
        ident = keep.tile([P, P], F32)
        make_identity(nc, ident[:])

        x_sb = keep.tile([P, D], BF16, align_bytes=64)
        nc.sync.dma_start(out=x_sb[:], in_=hidden_states)

        for quads in ((2, 3), (0, 1)):
            for j in range(3):
                for q in quads:
                    nc.sync.dma_start(
                        out=planes[32 * q : 32 * q + 16, j * E : (j + 1) * E].bitcast(I32),
                        in_=weight_scales[4 * j : 4 * j + 4, 4 * q : 4 * q + 4, :].bitcast(I32),
                    )

        def load_words(name, g, c0, width):
            wt = keep.tile([P, width], U32, name=name, align_bytes=64)
            nc.sync.dma_start(
                out=wt[:].bitcast(I32),
                in_=weight_words[g, :, c0 : c0 + width, :].rearrange("p n t -> p (n t)").bitcast(I32),
            )
            return wt

        whole = {}
        wide = {}
        narrow = {}
        last = {}
        for g in range(G_WHOLE):
            whole[g] = load_words("w%d" % g, g, 0, E)
        for g in range(G_WHOLE, G - 1):
            wide[g] = load_words("wa%d" % g, g, 0, SPLIT)
        for b in range(N_WIDE):
            last[b] = load_words("wl%d" % b, G - 1, BANKS[b][0], BANKS[b][1])
        for g in range(G_WHOLE, G - 1):
            narrow[g] = load_words("wb%d" % g, g, SPLIT, E - SPLIT)
        for b in range(N_WIDE, len(BANKS)):
            last[b] = load_words("wl%d" % b, G - 1, BANKS[b][0], BANKS[b][1])

        xw = x_sb[:].bitcast(F32)
        grouped = keep.tile([P, D], BF16, align_bytes=64)
        gw = grouped[:].bitcast(F32)
        x_codes = keep.tile([P, G * P], U32, align_bytes=64)
        x_scales = keep.tile([P, G * P], U8, align_bytes=64)

        def quantise(h):
            nc.vector.quantize_mx(
                out=x_codes[:, 512 * h : 512 * (h + 1)].bitcast(FP8X4),
                scales=x_scales[:, 512 * h : 512 * (h + 1)],
                in_=grouped[:, 2048 * h : 2048 * (h + 1)],
            )

        for b in range(6):
            tr = psum.tile([P, 512], F32, name="tr%d" % b, tag="b%d" % (6 + b % 2))
            for i in range(4):
                g = 2 * b + i // 2
                u = i % 2
                nc.tensor.transpose(
                    tr[:, 128 * i : 128 * (i + 1)],
                    xw[:, 256 * g + u : 256 * (g + 1) : 2],
                    ident[:],
                )
            src = tr[:].rearrange("p (g u t) -> p g t u", g=2, u=2)
            dst = gw[:, 512 * b : 512 * (b + 1)].rearrange("p (g t u) -> p g t u", g=2, u=2)
            if b % 2 == 0:
                nc.vector.tensor_copy(out=dst, in_=src)
            else:
                nc.scalar.copy(out=dst, in_=src)
            if b == 3 or b == 5:
                quantise((b - 3) // 2)
        quantise(2)

        acc = [
            psum.tile([P, BANKS[b][1]], F32, name="acc%d" % b, tag="b%d" % b) for b in range(len(BANKS))
        ]

        def mx_pass(g, b):
            c0, width = BANKS[b]
            if g < G_WHOLE:
                rhs = whole[g][:, c0 : c0 + width]
            elif g == G - 1:
                rhs = last[b][:]
            elif b < N_WIDE:
                rhs = wide[g][:, c0 : c0 + width]
            else:
                rhs = narrow[g][:, c0 - SPLIT : c0 - SPLIT + width]
            i = g % 4
            j = g // 4
            nc.tensor.matmul_mx(
                out=acc[b][:],
                lhsT=x_codes[:, P * g : P * (g + 1)].bitcast(FP8X4),
                lhsT_scale=x_scales[:, P * g : P * (g + 1)],
                rhs=rhs.bitcast(FP8X4),
                rhs_scale=planes[4 * i : P, j * E + c0 : j * E + c0 + width],
                start=(g == 0),
                stop=(g == G - 1),
            )

        for g in range(G_WHOLE):
            for b in range(len(BANKS)):
                mx_pass(g, b)
        for g in range(G_WHOLE, G):
            for b in range(N_WIDE):
                mx_pass(g, b)
        for g in range(G_WHOLE, G):
            for b in range(N_WIDE, len(BANKS)):
                mx_pass(g, b)

        for b in range(len(BANKS)):
            c0, width = BANKS[b]
            o = keep.tile([P, width], F32, name="o%d" % b)
            if b % 2 == 0:
                nc.vector.tensor_copy(out=o[:], in_=acc[b][:])
            else:
                nc.scalar.copy(out=o[:], in_=acc[b][:])
            nc.sync.dma_start(out=out[:, c0 : c0 + width], in_=o[:])
